import numpy as np
import ml_dtypes


def mxq(x, axis, fmt="e4m3"):
    dtype, down = {"e4m3": (ml_dtypes.float8_e4m3fn, 7), "e5m2": (ml_dtypes.float8_e5m2, 14)}[fmt]
    v = np.moveaxis(np.asarray(x, np.float32).astype(ml_dtypes.bfloat16).astype(np.float64), axis, -1)
    blocks = v.reshape(v.shape[:-1] + (-1, 32))
    amax = np.abs(blocks).max(-1, keepdims=True)
    byte = np.maximum(np.where(amax > 0, np.frexp(amax)[1] - 1 + 127, 0) - down, 1)
    scale = np.exp2(byte - 127.0)
    codes = (blocks / scale).astype(np.float32).astype(dtype).astype(np.float64)
    return np.moveaxis((codes * scale).reshape(v.shape), -1, axis)


WIDE = False


def mx_kscale(k):
    if not WIDE:
        return np.ones(k)
    levels = np.array([30, -30])
    if k % 512:
        return np.exp2(np.random.permutation(np.resize(levels, k // 32))).repeat(32)
    a = np.empty((k // 512, 16))
    for p in range(k // 512):
        a[p, :8] = np.random.permutation(np.resize(levels, 8))
        for g in range(8):
            far = levels[np.abs(levels - a[p, g]) >= 10]
            a[p, g + 8] = far[np.random.randint(len(far))]
    return np.exp2(a.ravel()).repeat(32)


BF16 = ml_dtypes.bfloat16


def bf(x):
    return np.asarray(x, np.float32).astype(BF16)


def f64(x):
    return np.asarray(x).astype(np.float64)


E2M1 = np.array([0.0, 0.5, 1.0, 1.5, 2.0, 3.0, 4.0, 6.0, -0.0, -0.5, -1.0, -1.5, -2.0, -3.0, -4.0, -6.0])


def pack_weight(w, fmt):
    k, n = w.shape
    w = f64(bf(w)).reshape(k // 32, 32, n)
    amax = np.abs(w).max(1)
    if fmt == "e4m3":
        byte = np.frexp(amax)[1] - 1 + 127 - 7
    else:
        mant, ex = np.frexp(amax / 6.0)
        byte = np.where(mant > 0.5, ex, ex - 1) + 127
    byte = np.clip(np.where(amax > 0, byte, 1), 1, 254)
    scaled = (w * np.exp2(127.0 - byte)[:, None, :]).reshape(k, n).astype(np.float32)
    by_word = np.ascontiguousarray(scaled.reshape(k // 512, 128, 4, n).transpose(0, 1, 3, 2))
    if fmt == "e4m3":
        words = by_word.astype(ml_dtypes.float8_e4m3fn).view(np.uint8)
    else:
        c = by_word.astype(ml_dtypes.float4_e2m1fn).view(np.uint8) & 0xF
        words = c[..., 0::2] | (c[..., 1::2] << 4)
    return np.ascontiguousarray(words), np.ascontiguousarray(byte.astype(np.uint8).reshape(k // 512, 16, n))


def unpack_weight(words, scales, fmt):
    g, p, n, _ = words.shape
    if fmt == "e4m3":
        vals = np.ascontiguousarray(words).view(ml_dtypes.float8_e4m3fn).astype(np.float64)
    else:
        nib = np.empty((g, p, n, 4), np.uint8)
        nib[..., 0::2] = words & 0xF
        nib[..., 1::2] = words >> 4
        vals = E2M1[nib]
    vals = vals * np.repeat(np.exp2(scales.astype(np.float64) - 127.0), 8, axis=1)[..., None]
    return vals.transpose(0, 1, 3, 2).reshape(g * 512, n)

def pack4(w):
    words, scales = pack_weight(w, "e2m1")
    return words.reshape(words.shape[0], 128, -1), scales


def unpack4(words, scales):
    return unpack_weight(words.reshape(words.shape[0], 128, -1, 2), scales, "e2m1")


B, T, D, H, HD = 2, 512, 1024, 8, 128
E = H * HD
HALF = HD // 2


def rotate_half(u):
    return np.concatenate((-u[..., HALF:], u[..., :HALF]), axis=-1)


def setup_inputs():
    s = mx_kscale(D)
    x = bf(np.random.standard_normal((B, T, D)) * s)
    rope_cos = bf(np.random.random_sample((1, 1, T, HD)))
    rope_sin = bf(np.random.random_sample((1, 1, T, HD)))
    w = np.random.standard_normal((3 * E, D)) / np.sqrt(D) / s[None, :]
    words, scales = pack4(np.ascontiguousarray(w.T))
    qkv_b = bf(np.random.standard_normal(3 * E) * 0.3)
    return {"x": x,
            "rope_cos": rope_cos,
            "rope_sin": rope_sin,
            "qkv_w_words": words,
            "qkv_w_scales": scales,
            "qkv_b": qkv_b}


def reference(x, rope_cos, rope_sin, qkv_w_words, qkv_w_scales, qkv_b):
    qkv = (mxq(f64(x), 2, "e5m2") @ unpack4(qkv_w_words, qkv_w_scales)) + f64(qkv_b)
    qkv = qkv.reshape(B, T, 3, H, HD).transpose(2, 0, 3, 1, 4)
    q, k, v = qkv[0], qkv[1], qkv[2]
    cos = f64(rope_cos)[:, :, :T, :]
    sin = f64(rope_sin)[:, :, :T, :]
    q_rot = q * cos + rotate_half(q) * sin
    k_rot = k * cos + rotate_half(k) * sin
    return q_rot, k_rot, v

@@ -1,0 +1,263 @@
+from contextlib import ExitStack
+
+import concourse.mybir as mybir
+from concourse.masks import make_identity
+
+B, T, D, H, HD = 2, 512, 1024, 8, 128
+HALF = HD // 2
+FLOPS = 2 * B * T * D * 3 * H * HD
+
+F32 = mybir.dt.float32
+BF16 = mybir.dt.bfloat16
+I32 = mybir.dt.int32
+U32 = mybir.dt.uint32
+U8 = mybir.dt.uint8
+E5M2X4 = mybir.dt.float8_e5m2_x4
+E2M1X4 = mybir.dt.float4_e2m1fn_x4
+ALU = mybir.AluOpType
+ACT = mybir.ActivationFunctionType
+
+P = 128
+PASSES = D // 512
+SLOTS = T // P
+BANK = 512
+HEADS = 3 * H
+V0 = 2 * H
+QUAD = 4
+ROUNDS = 2 * H // QUAD
+SPLIT = 12
+ROPE_QUADS = [SPLIT] + list(range(0, SPLIT, QUAD))
+X_STEPS = (1, 2)
+
+
+def tile_causalselfattention_pa_kernel(tc, x, rope_cos, rope_sin, w_words, w_scales, qkv_b, out_0, out_1, out_2):
+    nc = tc.nc
+    outs = (out_0, out_1, out_2)
+
+    with ExitStack() as ctx:
+        keep = ctx.enter_context(tc.tile_pool(name="keep", bufs=1))
+        work = ctx.enter_context(tc.tile_pool(name="work", bufs=1))
+        psum = ctx.enter_context(tc.psum_pool(name="psum", bufs=1))
+        ctx.enter_context(tc.manual_schedule())
+
+        def bank(kind, n):
+            return psum.tile([P, BANK], F32, tag=f"{kind}{n}", name=f"{kind}{n}")
+
+        bias_rows = keep.tile([P, 3, HD], BF16, name="bias_rows")
+        nc.gpsimd.memset(bias_rows[:].rearrange("p s d -> p (s d)").bitcast(I32), 0)
+        nc.scalar.dma_start(out=bias_rows[0:H, :, :], in_=qkv_b.rearrange("(s h d) -> h s d", s=3, h=H))
+
+        plane_heads = [(SPLIT, HEADS), (0, SPLIT)]
+        planes = []
+        for n, (lo, hi) in enumerate(plane_heads):
+            plane = keep.tile([P, PASSES, (hi - lo) * HD], U8, name=f"plane{n}", align_bytes=64)
+            nc.vector.memset(plane[:].rearrange("p g n -> p (g n)").bitcast(I32), 0)
+            planes.append(plane)
+
+        ident_bf = keep.tile([P, P], BF16, name="ident_bf")
+        make_identity(nc, ident_bf[:])
+        ident = keep.tile([P, P], F32, name="ident")
+        make_identity(nc, ident[:])
+
+        def load_x(b, j0, count):
+            raw = keep.tile([P, count, D], BF16, name=f"x_raw{b}_{j0}")
+            nc.sync.dma_start(out=raw[:], in_=x[b].rearrange("(p j) k -> p j k", j=SLOTS)[:, j0 : j0 + count, :])
+            return raw
+
+        def load_scales(n):
+            lo, hi = plane_heads[n]
+            for r in range(4):
+                nc.sync.dma_start(
+                    out=planes[n][r:P:32, :, :].bitcast(I32),
+                    in_=w_scales[:, r:16:4, lo * HD : hi * HD].rearrange("g q n -> q g n").bitcast(I32),
+                )
+
+        w_tiles = {}
+
+        def load_w(c0):
+            tile = keep.tile([P, PASSES, QUAD * HD * 2], U8, name=f"w{c0}", align_bytes=64)
+            nc.sync.dma_start(
+                out=tile[:].bitcast(I32),
+                in_=w_words[:, :, c0 * HD * 2 : (c0 + QUAD) * HD * 2].rearrange("g p n -> p g n").bitcast(I32),
+            )
+            w_tiles[c0] = tile
+
+        def w_operand(g, c, count):
+            c0 = c - c % QUAD
+            n = 0 if c >= SPLIT else 1
+            lo = plane_heads[n][0]
+            codes = w_tiles[c0][:, g, (c - c0) * HD * 2 : (c - c0 + count) * HD * 2].bitcast(E2M1X4)
+            return codes, planes[n][:, g, (c - lo) * HD : (c - lo + count) * HD]
+
+        x_first = [load_x(0, j, 1) for j in range(SLOTS)]
+        load_scales(0)
+        load_w(V0)
+        load_w(ROPE_QUADS[0])
+        table = keep.tile([P, 2, T // P * HD], BF16, name="table")
+        sin_raw = keep.tile([P, SLOTS, HD], BF16, name="sin_raw")
+        nc.sync.dma_start(out=table[:, 0, :], in_=rope_cos[0, 0].rearrange("(p j) d -> p (j d)", j=SLOTS))
+        nc.sync.dma_start(out=sin_raw[:], in_=rope_sin[0, 0].rearrange("(p j) d -> p j d", j=SLOTS))
+        load_scales(1)
+        load_w(ROPE_QUADS[1])
+        x_second = load_x(1, 0, SLOTS)
+        load_w(ROPE_QUADS[2])
+        load_w(V0 + QUAD)
+        load_w(ROPE_QUADS[3])
+
+        cols_ps = bank("mx", 0)
+        for s in range(3):
+            nc.tensor.matmul(cols_ps[:, s * H : (s + 1) * H], lhsT=bias_rows[:, s, :], rhs=ident_bf[:, 0:H], start=True, stop=True)
+        bias_cols = keep.tile([P, HEADS], F32, name="bias_cols")
+        nc.scalar.copy(out=bias_cols[:], in_=cols_ps[:, 0:HEADS])
+        v_bias = keep.tile([P, H * HD], F32, name="v_bias")
+        for half in range(2):
+            spread = bank("v", half)
+            for n in range(QUAD):
+                h = half * QUAD + n
+                nc.tensor.matmul(
+                    spread[:, n * HD : (n + 1) * HD],
+                    lhsT=ident_bf[:, h : h + 1].to_broadcast([P, P]),
+                    rhs=bias_rows[:, 2, :],
+                    start=True,
+                    stop=True,
+                )
+            nc.vector.tensor_copy(out=v_bias[:, half * BANK : (half + 1) * BANK], in_=spread[:])
+
+        x_codes = [keep.tile([P, PASSES, T], U32, name=f"x_codes{b}", align_bytes=64) for b in range(B)]
+        x_scales = [keep.tile([P, PASSES, T], U8, name=f"x_scales{b}", align_bytes=64) for b in range(B)]
+
+        def transpose_x(rows, jj, grouped, ps, copy):
+            words = rows.bitcast(F32)
+            for g in range(PASSES):
+                for u in range(2):
+                    n = 2 * g + u
+                    nc.tensor.transpose(ps[:, n * P : (n + 1) * P], words[:, 256 * g + u : 256 * (g + 1) : 2], ident[:])
+            dst = grouped[:].bitcast(F32).rearrange("p g (r u) -> p g r u", u=2)[:, :, jj * P : (jj + 1) * P, :]
+            copy(out=dst, in_=ps[:].rearrange("p (g u r) -> p g r u", g=PASSES, u=2))
+
+        for jp in range(2):
+            grouped = keep.tile([P, PASSES, 2 * P * 4], BF16, name=f"grouped0_{jp}", align_bytes=64)
+            transpose_x(x_first[2 * jp][:, 0, :], 0, grouped, bank("t", 2 * jp), nc.vector.tensor_copy)
+            transpose_x(x_first[2 * jp + 1][:, 0, :], 1, grouped, bank("t", 2 * jp + 1), nc.scalar.copy)
+            for g in range(PASSES):
+                cols = slice(jp * 2 * P, (jp + 1) * 2 * P)
+                nc.vector.quantize_mx(out=x_codes[0][:, g, cols].bitcast(E5M2X4), scales=x_scales[0][:, g, cols], in_=grouped[:, g, :])
+        grouped_second = keep.tile([P, PASSES, T * 4], BF16, name="grouped1", align_bytes=64)
+
+        sin_swapped = table[:, 1, :].rearrange("p (j d) -> p j d", d=HD)
+        nc.scalar.copy(out=sin_swapped[:, :, 0:HALF], in_=sin_raw[:, :, HALF:HD])
+        nc.scalar.copy(out=sin_swapped[:, :, HALF:HD], in_=sin_raw[:, :, 0:HALF])
+
+        def project_features(b, c, ps):
+            for g in range(PASSES):
+                codes, scales = w_operand(g, c, 1)
+                nc.tensor.matmul_mx(
+                    out=ps[:],
+                    lhsT=codes,
+                    lhsT_scale=scales,
+                    rhs=x_codes[b][:, g, :].bitcast(E5M2X4),
+                    rhs_scale=x_scales[b][:, g, :],
+                    start=(g == 0),
+                    stop=(g == PASSES - 1),
+                )
+            biased = work.tile([P, T], F32, name="biased", bufs=8)
+            nc.scalar.activation(out=biased[:], in_=ps[:], func=ACT.Identity, bias=bias_cols[:, c : c + 1])
+            return biased
+
+        def project_tokens(b, c, jp, ps):
+            for jj in range(2):
+                j = 2 * jp + jj
+                for g in range(PASSES):
+                    codes, scales = w_operand(g, c, 2)
+                    nc.tensor.matmul_mx(
+                        out=ps[:, jj * 2 * HD : (jj + 1) * 2 * HD],
+                        lhsT=x_codes[b][:, g, j * P : (j + 1) * P].bitcast(E5M2X4),
+                        lhsT_scale=x_scales[b][:, g, j * P : (j + 1) * P],
+                        rhs=codes,
+                        rhs_scale=scales,
+                        start=(g == 0),
+                        stop=(g == PASSES - 1),
+                    )
+            return ps
+
+        def to_tokens(biased, ps):
+            for j in range(SLOTS):
+                nc.tensor.transpose(ps[:, j * P : (j + 1) * P], biased[:, j * P : (j + 1) * P], ident[:])
+            return ps
+
+        def hbm_rows(b, c):
+            return outs[c // H][b, c % H : c % H + 2].rearrange("h (p j) d -> p h (j d)", j=SLOTS)
+
+        def add_v_bias(b, c, banks, split_store):
+            result = work.tile([P, 2, T], F32, name="v_result", bufs=3)
+            by_slot = result[:].rearrange("p h (j d) -> p j h d", d=HD)
+            bias = v_bias[:, (c - V0) * HD : (c - V0 + 2) * HD].rearrange("p (o h d) -> p o h d", o=1, h=2)
+            for jp in range(2):
+                nc.vector.tensor_tensor(
+                    out=by_slot[:, 2 * jp : 2 * jp + 2, :, :],
+                    in0=banks[jp][:].rearrange("p (j h d) -> p j h d", j=2, h=2),
+                    in1=bias.to_broadcast([P, 2, 2, HD]),
+                    op=ALU.add,
+                )
+                if split_store:
+                    cols = slice(jp * 2 * HD, (jp + 1) * 2 * HD)
+                    nc.sync.dma_start(out=hbm_rows(b, c)[:, :, cols], in_=result[:, :, cols])
+            if not split_store:
+                nc.sync.dma_start(out=hbm_rows(b, c), in_=result[:])
+
+        def rotate(b, c, banks):
+            products = work.tile([P, 2, 2, T], F32, name="products", bufs=3)
+            for n in range(2):
+                nc.vector.tensor_tensor(
+                    out=products[:, :, n, :],
+                    in0=banks[n][:].rearrange("p (o n) -> p o n", o=1).to_broadcast([P, 2, BANK]),
+                    in1=table[:],
+                    op=ALU.mult,
+                )
+            result = work.tile([P, 2, T], F32, name="rope_result", bufs=4)
+            rows = result[:].rearrange("p h (j d) -> p (h j) d", d=HD)
+            with_cos = products[:, 0, :, :].rearrange("p h (j d) -> p (h j) d", d=HD)
+            with_sin = products[:, 1, :, :].rearrange("p h (j d) -> p (h j) d", d=HD)
+            nc.gpsimd.tensor_tensor(out=rows[:, :, 0:HALF], in0=with_cos[:, :, 0:HALF], in1=with_sin[:, :, HALF:HD], op=ALU.subtract)
+            nc.gpsimd.tensor_tensor(out=rows[:, :, HALF:HD], in0=with_cos[:, :, HALF:HD], in1=with_sin[:, :, 0:HALF], op=ALU.add)
+            return result
+
+        last = B * ROUNDS - 1
+        for step in range(B * ROUNDS):
+            b, i = divmod(step, ROUNDS)
+            c0 = ROPE_QUADS[i]
+            has_v = step != ROUNDS
+            cv = V0 + 2 * (i - b)
+            biased, v_banks, t_banks = [], [], []
+            if step == 0:
+                v_banks.append(project_tokens(b, cv, 0, bank("v", 0)))
+                biased += [project_features(b, c0 + n, bank("mx", n)) for n in range(2)]
+                v_banks.append(project_tokens(b, cv, 1, bank("v", 1)))
+                t_banks += [to_tokens(biased[n], bank("t", n)) for n in range(2)]
+                biased += [project_features(b, c0 + 2 + n, bank("mx", n)) for n in range(2)]
+            else:
+                for half in range(2):
+                    biased += [project_features(b, c0 + 2 * half + n, bank("mx", n)) for n in range(2)]
+                    if has_v:
+                        v_banks.append(project_tokens(b, cv, half, bank("v", half)))
+            if step in X_STEPS:
+                for n in range(2):
+                    j = 2 * X_STEPS.index(step) + n
+                    transpose_x(x_second[:, j, :], j, grouped_second, bank("mx", n), nc.scalar.copy)
+            t_banks += [to_tokens(biased[n], bank("t", n)) for n in range(len(t_banks), QUAD)]
+            if has_v and step != last:
+                add_v_bias(b, cv, v_banks, False)
+            if step == X_STEPS[-1]:
+                nc.vector.quantize_mx(
+                    out=x_codes[1][:].rearrange("p g r -> p (g r)").bitcast(E5M2X4),
+                    scales=x_scales[1][:].rearrange("p g r -> p (g r)"),
+                    in_=grouped_second[:].rearrange("p g n -> p (g n)"),
+                )
+            if step == last:
+                final_banks = [project_tokens(b, cv + 2, half, bank("mx", half)) for half in range(2)]
+            for n in range(0, QUAD, 2):
+                rotated = rotate(b, c0 + n, t_banks[n : n + 2])
+                if step == last and n == 2:
+                    add_v_bias(b, cv, v_banks, False)
+                    add_v_bias(b, cv + 2, final_banks, True)
+                nc.sync.dma_start(out=hbm_rows(b, c0 + n), in_=rotated[:])

@@ -27,7 +27,10 @@ QUAD = 4
 ROUNDS = 2 * H // QUAD
 SPLIT = 12
 ROPE_QUADS = [SPLIT] + list(range(0, SPLIT, QUAD))
-X_STEPS = (1, 2)
+X_STEPS = (0, 1)
+QUANT_STEP = 2
+GPSIMD_V_STEPS = (0, 1, 4, 5)
+DOUBLE_V_STEP = 4
 
 
 def tile_causalselfattention_pa_kernel(tc, x, rope_cos, rope_sin, w_words, w_scales, qkv_b, out_0, out_1, out_2):
@@ -54,10 +57,13 @@ def tile_causalselfattention_pa_kernel(tc, x, rope_cos, rope_sin, w_words, w_sca
             nc.vector.memset(plane[:].rearrange("p g n -> p (g n)").bitcast(I32), 0)
             planes.append(plane)
 
-        ident_bf = keep.tile([P, P], BF16, name="ident_bf")
-        make_identity(nc, ident_bf[:])
         ident = keep.tile([P, P], F32, name="ident")
         make_identity(nc, ident[:])
+        ident_bf = keep.tile([P, P], BF16, name="ident_bf")
+        make_identity(nc, ident_bf[:])
+        half_swap = keep.tile([P, P], F32, name="half_swap")
+        nc.scalar.copy(out=half_swap[:, 0:HALF], in_=ident[:, HALF:HD])
+        nc.scalar.copy(out=half_swap[:, HALF:HD], in_=ident[:, 0:HALF])
 
         def load_x(b, j0, count):
             raw = keep.tile([P, count, D], BF16, name=f"x_raw{b}_{j0}")
@@ -90,16 +96,17 @@ def tile_causalselfattention_pa_kernel(tc, x, rope_cos, rope_sin, w_words, w_sca
             return codes, planes[n][:, g, (c - lo) * HD : (c - lo + count) * HD]
 
         x_first = [load_x(0, j, 1) for j in range(SLOTS)]
-        load_scales(0)
-        load_w(V0)
-        load_w(ROPE_QUADS[0])
         table = keep.tile([P, 2, T // P * HD], BF16, name="table")
         sin_raw = keep.tile([P, SLOTS, HD], BF16, name="sin_raw")
-        nc.sync.dma_start(out=table[:, 0, :], in_=rope_cos[0, 0].rearrange("(p j) d -> p (j d)", j=SLOTS))
         nc.sync.dma_start(out=sin_raw[:], in_=rope_sin[0, 0].rearrange("(p j) d -> p j d", j=SLOTS))
+        nc.sync.dma_start(out=table[:, 0, :], in_=rope_cos[0, 0].rearrange("(p j) d -> p (j d)", j=SLOTS))
+        load_scales(0)
+        load_w(ROPE_QUADS[0])
+        load_w(V0)
+        x_second = [load_x(1, 0, 2)]
         load_scales(1)
         load_w(ROPE_QUADS[1])
-        x_second = load_x(1, 0, SLOTS)
+        x_second.append(load_x(1, 2, 2))
         load_w(ROPE_QUADS[2])
         load_w(V0 + QUAD)
         load_w(ROPE_QUADS[3])
@@ -108,20 +115,23 @@ def tile_causalselfattention_pa_kernel(tc, x, rope_cos, rope_sin, w_words, w_sca
         for s in range(3):
             nc.tensor.matmul(cols_ps[:, s * H : (s + 1) * H], lhsT=bias_rows[:, s, :], rhs=ident_bf[:, 0:H], start=True, stop=True)
         bias_cols = keep.tile([P, HEADS], F32, name="bias_cols")
-        nc.scalar.copy(out=bias_cols[:], in_=cols_ps[:, 0:HEADS])
-        v_bias = keep.tile([P, H * HD], F32, name="v_bias")
-        for half in range(2):
-            spread = bank("v", half)
+        nc.vector.tensor_copy(out=bias_cols[:], in_=cols_ps[:, 0:HEADS])
+        v_bias = [keep.tile([P, QUAD * HD], F32, name=f"v_bias{half}") for half in range(2)]
+
+        def spread_v_bias(half, ps):
             for n in range(QUAD):
                 h = half * QUAD + n
                 nc.tensor.matmul(
-                    spread[:, n * HD : (n + 1) * HD],
+                    ps[:, n * HD : (n + 1) * HD],
                     lhsT=ident_bf[:, h : h + 1].to_broadcast([P, P]),
                     rhs=bias_rows[:, 2, :],
                     start=True,
                     stop=True,
                 )
-            nc.vector.tensor_copy(out=v_bias[:, half * BANK : (half + 1) * BANK], in_=spread[:])
+            nc.vector.tensor_copy(out=v_bias[half][:], in_=ps[:])
+
+        for half in range(2):
+            spread_v_bias(half, bank("v", half))
 
         x_codes = [keep.tile([P, PASSES, T], U32, name=f"x_codes{b}", align_bytes=64) for b in range(B)]
         x_scales = [keep.tile([P, PASSES, T], U8, name=f"x_scales{b}", align_bytes=64) for b in range(B)]
@@ -135,18 +145,29 @@ def tile_causalselfattention_pa_kernel(tc, x, rope_cos, rope_sin, w_words, w_sca
             dst = grouped[:].bitcast(F32).rearrange("p g (r u) -> p g r u", u=2)[:, :, jj * P : (jj + 1) * P, :]
             copy(out=dst, in_=ps[:].rearrange("p (g u r) -> p g r u", g=PASSES, u=2))
 
+        def quantize_first(jp, grouped):
+            cols = slice(jp * 2 * P, (jp + 1) * 2 * P)
+            for g in range(PASSES):
+                nc.vector.quantize_mx(out=x_codes[0][:, g, cols].bitcast(E5M2X4), scales=x_scales[0][:, g, cols], in_=grouped[:, g, :])
+
         for jp in range(2):
             grouped = keep.tile([P, PASSES, 2 * P * 4], BF16, name=f"grouped0_{jp}", align_bytes=64)
-            transpose_x(x_first[2 * jp][:, 0, :], 0, grouped, bank("t", 2 * jp), nc.vector.tensor_copy)
-            transpose_x(x_first[2 * jp + 1][:, 0, :], 1, grouped, bank("t", 2 * jp + 1), nc.scalar.copy)
-            for g in range(PASSES):
-                cols = slice(jp * 2 * P, (jp + 1) * 2 * P)
-                nc.vector.quantize_mx(out=x_codes[0][:, g, cols].bitcast(E5M2X4), scales=x_scales[0][:, g, cols], in_=grouped[:, g, :])
+            transpose_x(x_first[2 * jp][:, 0, :], 0, grouped, bank("f", jp), nc.vector.tensor_copy)
+            transpose_x(x_first[2 * jp + 1][:, 0, :], 1, grouped, bank("t", jp), nc.scalar.copy)
+            quantize_first(jp, grouped)
+            if jp == 0:
+                sin_swapped = table[:, 1, :].rearrange("p (j d) -> p j d", d=HD)
+                nc.scalar.copy(out=sin_swapped[:, :, 0:HALF], in_=sin_raw[:, :, HALF:HD])
+                nc.scalar.activation(out=sin_swapped[:, :, HALF:HD], in_=sin_raw[:, :, 0:HALF], func=ACT.Copy, scale=-1.0)
         grouped_second = keep.tile([P, PASSES, T * 4], BF16, name="grouped1", align_bytes=64)
 
-        sin_swapped = table[:, 1, :].rearrange("p (j d) -> p j d", d=HD)
-        nc.scalar.copy(out=sin_swapped[:, :, 0:HALF], in_=sin_raw[:, :, HALF:HD])
-        nc.scalar.copy(out=sin_swapped[:, :, HALF:HD], in_=sin_raw[:, :, 0:HALF])
+        table_ps = psum.tile([P, 2, T], BF16, tag="mx1", name="table_ps")
+        for w in range(2):
+            for j in range(SLOTS):
+                nc.tensor.transpose(table_ps[:, w, j * P : (j + 1) * P], table[:, w, j * HD : (j + 1) * HD], ident_bf[:])
+        table_features = keep.tile([P, 2, T], BF16, name="table_features")
+        nc.scalar.copy(out=table_features[:], in_=table_ps[:])
+
 
         def project_features(b, c, ps):
             for g in range(PASSES):
@@ -160,9 +181,7 @@ def tile_causalselfattention_pa_kernel(tc, x, rope_cos, rope_sin, w_words, w_sca
                     start=(g == 0),
                     stop=(g == PASSES - 1),
                 )
-            biased = work.tile([P, T], F32, name="biased", bufs=8)
-            nc.scalar.activation(out=biased[:], in_=ps[:], func=ACT.Identity, bias=bias_cols[:, c : c + 1])
-            return biased
+            return ps
 
         def project_tokens(b, c, jp, ps):
             for jj in range(2):
@@ -180,84 +199,131 @@ def tile_causalselfattention_pa_kernel(tc, x, rope_cos, rope_sin, w_words, w_sca
                     )
             return ps
 
+        def twice(ps):
+            return ps[:].rearrange("p (o n) -> p o n", o=1).to_broadcast([P, 2, BANK])
+
+        def hbm_rows(b, c, count):
+            return outs[c // H][b, c % H : c % H + count].rearrange("h (p j) d -> p h (j d)", j=SLOTS)
+
+        def add_bias(c, ps):
+            biased = work.tile([P, T], F32, name="biased", bufs=4)
+            nc.scalar.activation(out=biased[:], in_=ps[:], func=ACT.Identity, bias=bias_cols[:, c : c + 1])
+            return biased
+
         def to_tokens(biased, ps):
             for j in range(SLOTS):
                 nc.tensor.transpose(ps[:, j * P : (j + 1) * P], biased[:, j * P : (j + 1) * P], ident[:])
             return ps
 
-        def hbm_rows(b, c):
-            return outs[c // H][b, c % H : c % H + 2].rearrange("h (p j) d -> p h (j d)", j=SLOTS)
-
-        def add_v_bias(b, c, banks, split_store):
-            result = work.tile([P, 2, T], F32, name="v_result", bufs=3)
-            by_slot = result[:].rearrange("p h (j d) -> p j h d", d=HD)
-            bias = v_bias[:, (c - V0) * HD : (c - V0 + 2) * HD].rearrange("p (o h d) -> p o h d", o=1, h=2)
-            for jp in range(2):
-                nc.vector.tensor_tensor(
-                    out=by_slot[:, 2 * jp : 2 * jp + 2, :, :],
-                    in0=banks[jp][:].rearrange("p (j h d) -> p j h d", j=2, h=2),
-                    in1=bias.to_broadcast([P, 2, 2, HD]),
-                    op=ALU.add,
-                )
-                if split_store:
-                    cols = slice(jp * 2 * HD, (jp + 1) * 2 * HD)
-                    nc.sync.dma_start(out=hbm_rows(b, c)[:, :, cols], in_=result[:, :, cols])
-            if not split_store:
-                nc.sync.dma_start(out=hbm_rows(b, c), in_=result[:])
-
-        def rotate(b, c, banks):
+        def rotate_tokens(b, c, banks):
             products = work.tile([P, 2, 2, T], F32, name="products", bufs=3)
             for n in range(2):
-                nc.vector.tensor_tensor(
-                    out=products[:, :, n, :],
-                    in0=banks[n][:].rearrange("p (o n) -> p o n", o=1).to_broadcast([P, 2, BANK]),
-                    in1=table[:],
-                    op=ALU.mult,
-                )
-            result = work.tile([P, 2, T], F32, name="rope_result", bufs=4)
+                nc.vector.tensor_tensor(out=products[:, :, n, :], in0=twice(banks[n]), in1=table[:], op=ALU.mult)
+            result = work.tile([P, 2, T], F32, name="rope_result", bufs=3)
             rows = result[:].rearrange("p h (j d) -> p (h j) d", d=HD)
             with_cos = products[:, 0, :, :].rearrange("p h (j d) -> p (h j) d", d=HD)
             with_sin = products[:, 1, :, :].rearrange("p h (j d) -> p (h j) d", d=HD)
-            nc.gpsimd.tensor_tensor(out=rows[:, :, 0:HALF], in0=with_cos[:, :, 0:HALF], in1=with_sin[:, :, HALF:HD], op=ALU.subtract)
+            nc.gpsimd.tensor_tensor(out=rows[:, :, 0:HALF], in0=with_cos[:, :, 0:HALF], in1=with_sin[:, :, HALF:HD], op=ALU.add)
             nc.gpsimd.tensor_tensor(out=rows[:, :, HALF:HD], in0=with_cos[:, :, HALF:HD], in1=with_sin[:, :, 0:HALF], op=ALU.add)
-            return result
+            nc.sync.dma_start(out=hbm_rows(b, c, 2), in_=result[:])
+
+        def multiply_features(c, ps):
+            products = work.tile([P, 2, T], F32, name="feature_products", bufs=6)
+            nc.vector.scalar_tensor_tensor(
+                out=products[:], in0=twice(ps), scalar=bias_cols[:, c : c + 1], in1=table_features[:], op0=ALU.add, op1=ALU.mult
+            )
+            return products
+
+        def sum_to_tokens(products, ps, result):
+            for j in range(SLOTS):
+                cols = slice(j * P, (j + 1) * P)
+                nc.tensor.matmul(ps[:, cols], lhsT=products[:, 0, cols], rhs=ident[:], is_transpose=True, start=True, stop=False)
+                nc.tensor.matmul(ps[:, cols], lhsT=products[:, 1, cols], rhs=half_swap[:], is_transpose=True, start=False, stop=True)
+            nc.scalar.copy(out=result, in_=ps[:])
+
+        def by_slot(tile):
+            return tile[:].rearrange("p h (j d) -> p j h d", d=HD)
+
+        def slots_of(ps):
+            return ps[:].rearrange("p (j h d) -> p j h d", j=2, h=2)
+
+        def pair_bias(c):
+            half, n = divmod(c - V0, QUAD)
+            return v_bias[half][:, n * HD : (n + 2) * HD]
+
+        def v_pair(b, c, on_gpsimd):
+            result = work.tile([P, 2, T], F32, name="v_result", bufs=3)
+            banks = []
+            if on_gpsimd:
+                plain = work.tile([P, 2, T], F32, name="v_plain", bufs=2)
+
+            def project(jp):
+                banks.append(project_tokens(b, c, jp, bank("v", jp)))
+                if on_gpsimd:
+                    nc.scalar.copy(out=by_slot(plain)[:, 2 * jp : 2 * jp + 2, :, :], in_=slots_of(banks[jp]))
+
+            def finish():
+                if on_gpsimd:
+                    nc.gpsimd.tensor_tensor(
+                        out=result[:].rearrange("p h (j d) -> p h j d", d=HD),
+                        in0=plain[:].rearrange("p h (j d) -> p h j d", d=HD),
+                        in1=pair_bias(c).rearrange("p (h o d) -> p h o d", h=2, o=1).to_broadcast([P, 2, SLOTS, HD]),
+                        op=ALU.add,
+                    )
+                else:
+                    bias = pair_bias(c).rearrange("p (o h d) -> p o h d", o=1, h=2).to_broadcast([P, 2, 2, HD])
+                    for jp in range(2):
+                        nc.vector.tensor_tensor(out=by_slot(result)[:, 2 * jp : 2 * jp + 2, :, :], in0=slots_of(banks[jp]), in1=bias, op=ALU.add)
+                nc.sync.dma_start(out=hbm_rows(b, c, 2), in_=result[:])
+
+            return project, finish
 
         last = B * ROUNDS - 1
-        for step in range(B * ROUNDS):
+        v_pairs = [(b, V0 + 2 * i) for b in range(B) for i in range(ROUNDS)]
+        waiting = []
+        for step in range(last):
             b, i = divmod(step, ROUNDS)
             c0 = ROPE_QUADS[i]
-            has_v = step != ROUNDS
-            cv = V0 + 2 * (i - b)
-            biased, v_banks, t_banks = [], [], []
-            if step == 0:
-                v_banks.append(project_tokens(b, cv, 0, bank("v", 0)))
-                biased += [project_features(b, c0 + n, bank("mx", n)) for n in range(2)]
-                v_banks.append(project_tokens(b, cv, 1, bank("v", 1)))
-                t_banks += [to_tokens(biased[n], bank("t", n)) for n in range(2)]
-                biased += [project_features(b, c0 + 2 + n, bank("mx", n)) for n in range(2)]
-            else:
-                for half in range(2):
-                    biased += [project_features(b, c0 + 2 * half + n, bank("mx", n)) for n in range(2)]
-                    if has_v:
-                        v_banks.append(project_tokens(b, cv, half, bank("v", half)))
+            project_v, finish_v = v_pair(*v_pairs.pop(0), step in GPSIMD_V_STEPS)
+            fresh = [multiply_features(c0 + n, project_features(b, c0 + n, bank("f", n))) for n in range(2)]
+            project_v(0)
+            if step == DOUBLE_V_STEP:
+                project_v(1)
+                finish_v()
+                project_v, finish_v = v_pair(*v_pairs.pop(0), False)
+            biased = [add_bias(c0 + 2 + n, project_features(b, c0 + 2 + n, bank("mx", n))) for n in range(2)]
+            if step == DOUBLE_V_STEP:
+                project_v(0)
+            project_v(1)
+
+            t_banks = []
+            if waiting:
+                summed = work.tile([P, 2, T], F32, name="summed", bufs=3)
+            for n in range(2):
+                t_banks.append(to_tokens(biased[n], bank("t", n)))
+                if waiting:
+                    sum_to_tokens(waiting[n], bank("mx", n), summed[:, n, :])
+            if waiting:
+                nc.sync.dma_start(out=hbm_rows(*waiting_rows, 2), in_=summed[:])
+            waiting, waiting_rows = fresh, (b, c0)
             if step in X_STEPS:
-                for n in range(2):
-                    j = 2 * X_STEPS.index(step) + n
-                    transpose_x(x_second[:, j, :], j, grouped_second, bank("mx", n), nc.scalar.copy)
-            t_banks += [to_tokens(biased[n], bank("t", n)) for n in range(len(t_banks), QUAD)]
-            if has_v and step != last:
-                add_v_bias(b, cv, v_banks, False)
-            if step == X_STEPS[-1]:
+                jp = X_STEPS.index(step)
+                for jj in range(2):
+                    transpose_x(x_second[jp][:, jj, :], 2 * jp + jj, grouped_second, bank("v", jj), nc.scalar.copy)
+            finish_v()
+            if step == QUANT_STEP:
                 nc.vector.quantize_mx(
                     out=x_codes[1][:].rearrange("p g r -> p (g r)").bitcast(E5M2X4),
                     scales=x_scales[1][:].rearrange("p g r -> p (g r)"),
                     in_=grouped_second[:].rearrange("p g n -> p (g n)"),
                 )
-            if step == last:
-                final_banks = [project_tokens(b, cv + 2, half, bank("mx", half)) for half in range(2)]
-            for n in range(0, QUAD, 2):
-                rotated = rotate(b, c0 + n, t_banks[n : n + 2])
-                if step == last and n == 2:
-                    add_v_bias(b, cv, v_banks, False)
-                    add_v_bias(b, cv + 2, final_banks, True)
-                nc.sync.dma_start(out=hbm_rows(b, c0 + n), in_=rotated[:])
+            rotate_tokens(b, c0 + 2, t_banks)
+
+        b, c0 = B - 1, ROPE_QUADS[-1]
+        places = [("f", 0), ("f", 1), ("v", 0), ("v", 1)]
+        fresh = [multiply_features(c0 + n, project_features(b, c0 + n, bank(*places[n]))) for n in range(QUAD)]
+        heads = [(waiting_rows[1] + n, waiting[n], ("mx", n)) for n in range(2)] + [(c0 + n, fresh[n], places[n]) for n in range(QUAD)]
+        for c, products, place in heads:
+            summed_head = work.tile([P, 1, T], F32, name="summed_head", bufs=len(heads))
+            sum_to_tokens(products, bank(*place), summed_head[:, 0, :])
+            nc.sync.dma_start(out=hbm_rows(b, c, 1), in_=summed_head[:])

@@ -18,19 +18,20 @@ ALU = mybir.AluOpType
 ACT = mybir.ActivationFunctionType
 
 P = 128
-PASSES = D // 512
+PACK = 4
+PASSES = D // (P * PACK)
+WORDS = D // PASSES // 2
 SLOTS = T // P
 BANK = 512
+W_BYTES = 2 * HD
 HEADS = 3 * H
 V0 = 2 * H
 QUAD = 4
-ROUNDS = 2 * H // QUAD
-SPLIT = 12
-ROPE_QUADS = [SPLIT] + list(range(0, SPLIT, QUAD))
-X_STEPS = (0, 1)
-QUANT_STEP = 2
-GPSIMD_V_STEPS = (0, 1, 4, 5)
-DOUBLE_V_STEP = 4
+STEPS = V0 // QUAD
+FIRST = V0 - QUAD
+QUADS = [FIRST] + list(range(0, FIRST, QUAD))
+PLANE_HEADS = [(FIRST, V0 + 2), (0, FIRST), (V0 + 2, HEADS)]
+X_STEPS = 2
 
 
 def tile_causalselfattention_pa_kernel(tc, x, rope_cos, rope_sin, w_words, w_scales, qkv_b, out_0, out_1, out_2):
@@ -43,20 +44,17 @@ def tile_causalselfattention_pa_kernel(tc, x, rope_cos, rope_sin, w_words, w_sca
         psum = ctx.enter_context(tc.psum_pool(name="psum", bufs=1))
         ctx.enter_context(tc.manual_schedule())
 
-        def bank(kind, n):
-            return psum.tile([P, BANK], F32, tag=f"{kind}{n}", name=f"{kind}{n}")
+        def bank(role, n):
+            return psum.tile([P, BANK], F32, tag=f"{role}{n}", name=f"{role}{n}")
 
         bias_rows = keep.tile([P, 3, HD], BF16, name="bias_rows")
         nc.gpsimd.memset(bias_rows[:].rearrange("p s d -> p (s d)").bitcast(I32), 0)
         nc.scalar.dma_start(out=bias_rows[0:H, :, :], in_=qkv_b.rearrange("(s h d) -> h s d", s=3, h=H))
-
-        plane_heads = [(SPLIT, HEADS), (0, SPLIT)]
         planes = []
-        for n, (lo, hi) in enumerate(plane_heads):
+        for n, (lo, hi) in enumerate(PLANE_HEADS):
             plane = keep.tile([P, PASSES, (hi - lo) * HD], U8, name=f"plane{n}", align_bytes=64)
             nc.vector.memset(plane[:].rearrange("p g n -> p (g n)").bitcast(I32), 0)
             planes.append(plane)
-
         ident = keep.tile([P, P], F32, name="ident")
         make_identity(nc, ident[:])
         ident_bf = keep.tile([P, P], BF16, name="ident_bf")
@@ -65,13 +63,13 @@ def tile_causalselfattention_pa_kernel(tc, x, rope_cos, rope_sin, w_words, w_sca
         nc.scalar.copy(out=half_swap[:, 0:HALF], in_=ident[:, HALF:HD])
         nc.scalar.copy(out=half_swap[:, HALF:HD], in_=ident[:, 0:HALF])
 
-        def load_x(b, j0, count):
-            raw = keep.tile([P, count, D], BF16, name=f"x_raw{b}_{j0}")
-            nc.sync.dma_start(out=raw[:], in_=x[b].rearrange("(p j) k -> p j k", j=SLOTS)[:, j0 : j0 + count, :])
+        def load_x(b, j, count):
+            raw = keep.tile([P, count, D], BF16, name=f"x_raw{b}_{j}")
+            nc.sync.dma_start(out=raw[:], in_=x[b].rearrange("(p j) k -> p j k", j=SLOTS)[:, j : j + count, :])
             return raw
 
         def load_scales(n):
-            lo, hi = plane_heads[n]
+            lo, hi = PLANE_HEADS[n]
             for r in range(4):
                 nc.sync.dma_start(
                     out=planes[n][r:P:32, :, :].bitcast(I32),
@@ -81,93 +79,92 @@ def tile_causalselfattention_pa_kernel(tc, x, rope_cos, rope_sin, w_words, w_sca
         w_tiles = {}
 
         def load_w(c0):
-            tile = keep.tile([P, PASSES, QUAD * HD * 2], U8, name=f"w{c0}", align_bytes=64)
+            w_tiles[c0] = keep.tile([P, PASSES, QUAD * W_BYTES], U8, name=f"w{c0}", align_bytes=64)
             nc.sync.dma_start(
-                out=tile[:].bitcast(I32),
-                in_=w_words[:, :, c0 * HD * 2 : (c0 + QUAD) * HD * 2].rearrange("g p n -> p g n").bitcast(I32),
+                out=w_tiles[c0][:].bitcast(I32),
+                in_=w_words[:, :, c0 * W_BYTES : (c0 + QUAD) * W_BYTES].rearrange("g p n -> p g n").bitcast(I32),
             )
-            w_tiles[c0] = tile
 
         def w_operand(g, c, count):
             c0 = c - c % QUAD
-            n = 0 if c >= SPLIT else 1
-            lo = plane_heads[n][0]
-            codes = w_tiles[c0][:, g, (c - c0) * HD * 2 : (c - c0 + count) * HD * 2].bitcast(E2M1X4)
+            n = [lo <= c < hi for lo, hi in PLANE_HEADS].index(True)
+            lo = PLANE_HEADS[n][0]
+            codes = w_tiles[c0][:, g, (c - c0) * W_BYTES : (c - c0 + count) * W_BYTES].bitcast(E2M1X4)
             return codes, planes[n][:, g, (c - lo) * HD : (c - lo + count) * HD]
 
         x_first = [load_x(0, j, 1) for j in range(SLOTS)]
-        table = keep.tile([P, 2, T // P * HD], BF16, name="table")
+        table = keep.tile([P, 2, SLOTS * HD], BF16, name="table")
         sin_raw = keep.tile([P, SLOTS, HD], BF16, name="sin_raw")
         nc.sync.dma_start(out=sin_raw[:], in_=rope_sin[0, 0].rearrange("(p j) d -> p j d", j=SLOTS))
         nc.sync.dma_start(out=table[:, 0, :], in_=rope_cos[0, 0].rearrange("(p j) d -> p (j d)", j=SLOTS))
         load_scales(0)
-        load_w(ROPE_QUADS[0])
+        load_w(QUADS[0])
         load_w(V0)
         x_second = [load_x(1, 0, 2)]
         load_scales(1)
-        load_w(ROPE_QUADS[1])
+        load_scales(2)
+        load_w(QUADS[1])
         x_second.append(load_x(1, 2, 2))
-        load_w(ROPE_QUADS[2])
+        load_w(QUADS[2])
         load_w(V0 + QUAD)
-        load_w(ROPE_QUADS[3])
+        load_w(QUADS[3])
 
-        cols_ps = bank("mx", 0)
+        cols_ps = bank("s", 0)
         for s in range(3):
             nc.tensor.matmul(cols_ps[:, s * H : (s + 1) * H], lhsT=bias_rows[:, s, :], rhs=ident_bf[:, 0:H], start=True, stop=True)
         bias_cols = keep.tile([P, HEADS], F32, name="bias_cols")
         nc.vector.tensor_copy(out=bias_cols[:], in_=cols_ps[:, 0:HEADS])
-        v_bias = [keep.tile([P, QUAD * HD], F32, name=f"v_bias{half}") for half in range(2)]
-
-        def spread_v_bias(half, ps):
-            for n in range(QUAD):
-                h = half * QUAD + n
-                nc.tensor.matmul(
-                    ps[:, n * HD : (n + 1) * HD],
-                    lhsT=ident_bf[:, h : h + 1].to_broadcast([P, P]),
-                    rhs=bias_rows[:, 2, :],
-                    start=True,
-                    stop=True,
-                )
-            nc.vector.tensor_copy(out=v_bias[half][:], in_=ps[:])
-
-        for half in range(2):
-            spread_v_bias(half, bank("v", half))
 
         x_codes = [keep.tile([P, PASSES, T], U32, name=f"x_codes{b}", align_bytes=64) for b in range(B)]
         x_scales = [keep.tile([P, PASSES, T], U8, name=f"x_scales{b}", align_bytes=64) for b in range(B)]
 
-        def transpose_x(rows, jj, grouped, ps, copy):
+        def transpose_x(rows, grouped, ps, copy):
             words = rows.bitcast(F32)
             for g in range(PASSES):
                 for u in range(2):
                     n = 2 * g + u
-                    nc.tensor.transpose(ps[:, n * P : (n + 1) * P], words[:, 256 * g + u : 256 * (g + 1) : 2], ident[:])
-            dst = grouped[:].bitcast(F32).rearrange("p g (r u) -> p g r u", u=2)[:, :, jj * P : (jj + 1) * P, :]
-            copy(out=dst, in_=ps[:].rearrange("p (g u r) -> p g r u", g=PASSES, u=2))
+                    nc.tensor.transpose(ps[:, n * P : (n + 1) * P], words[:, WORDS * g + u : WORDS * (g + 1) : 2], ident[:])
+            copy(out=grouped, in_=ps[:].rearrange("p (g u r) -> p g r u", g=PASSES, u=2))
 
-        def quantize_first(jp, grouped):
-            cols = slice(jp * 2 * P, (jp + 1) * 2 * P)
+        def as_words(grouped):
+            return grouped[:].bitcast(F32).rearrange("p g (r u) -> p g r u", u=2)
+
+        grouped_first = [keep.tile([P, PASSES, P * PACK], BF16, name=f"grouped0_{j}", align_bytes=64) for j in range(SLOTS)]
+
+        def quantize_first(j):
+            cols = slice(j * P, (j + 1) * P)
             for g in range(PASSES):
-                nc.vector.quantize_mx(out=x_codes[0][:, g, cols].bitcast(E5M2X4), scales=x_scales[0][:, g, cols], in_=grouped[:, g, :])
+                nc.vector.quantize_mx(
+                    out=x_codes[0][:, g, cols].bitcast(E5M2X4), scales=x_scales[0][:, g, cols], in_=grouped_first[j][:, g, :]
+                )
 
-        for jp in range(2):
-            grouped = keep.tile([P, PASSES, 2 * P * 4], BF16, name=f"grouped0_{jp}", align_bytes=64)
-            transpose_x(x_first[2 * jp][:, 0, :], 0, grouped, bank("f", jp), nc.vector.tensor_copy)
-            transpose_x(x_first[2 * jp + 1][:, 0, :], 1, grouped, bank("t", jp), nc.scalar.copy)
-            quantize_first(jp, grouped)
-            if jp == 0:
-                sin_swapped = table[:, 1, :].rearrange("p (j d) -> p j d", d=HD)
-                nc.scalar.copy(out=sin_swapped[:, :, 0:HALF], in_=sin_raw[:, :, HALF:HD])
-                nc.scalar.activation(out=sin_swapped[:, :, HALF:HD], in_=sin_raw[:, :, 0:HALF], func=ACT.Copy, scale=-1.0)
-        grouped_second = keep.tile([P, PASSES, T * 4], BF16, name="grouped1", align_bytes=64)
+        for j in range(SLOTS):
+            copy = nc.scalar.copy if j % 2 else nc.vector.tensor_copy
+            transpose_x(x_first[j][:, 0, :], as_words(grouped_first[j]), bank("t" if j % 2 else "f", j // 2), copy)
+            if j > 0:
+                quantize_first(j - 1)
+            if j == 1:
+                swapped = table[:, 1, :].rearrange("p (j d) -> p j d", d=HD)
+                nc.scalar.copy(out=swapped[:, :, 0:HALF], in_=sin_raw[:, :, HALF:HD])
+                nc.scalar.activation(out=swapped[:, :, HALF:HD], in_=sin_raw[:, :, 0:HALF], func=ACT.Copy, scale=-1.0)
+        quantize_first(SLOTS - 1)
+        grouped_second = keep.tile([P, PASSES, T * PACK], BF16, name="grouped1", align_bytes=64)
 
-        table_ps = psum.tile([P, 2, T], BF16, tag="mx1", name="table_ps")
-        for w in range(2):
+        table_ps = psum.tile([P, 2, T], BF16, tag="s1", name="table_ps")
+        for n in range(2):
             for j in range(SLOTS):
-                nc.tensor.transpose(table_ps[:, w, j * P : (j + 1) * P], table[:, w, j * HD : (j + 1) * HD], ident_bf[:])
+                nc.tensor.transpose(table_ps[:, n, j * P : (j + 1) * P], table[:, n, j * HD : (j + 1) * HD], ident_bf[:])
         table_features = keep.tile([P, 2, T], BF16, name="table_features")
         nc.scalar.copy(out=table_features[:], in_=table_ps[:])
-
+        v_bias = []
+        for half in range(2):
+            spread = bank("t", half)
+            for n in range(QUAD):
+                h = half * QUAD + n
+                picker = ident_bf[:, h : h + 1].to_broadcast([P, P])
+                nc.tensor.matmul(spread[:, n * HD : (n + 1) * HD], lhsT=picker, rhs=bias_rows[:, 2, :], start=True, stop=True)
+            v_bias.append(keep.tile([P, QUAD * HD], F32, name=f"v_bias{half}"))
+            nc.scalar.copy(out=v_bias[half][:], in_=spread[:])
 
         def project_features(b, c, ps):
             for g in range(PASSES):
@@ -184,14 +181,14 @@ def tile_causalselfattention_pa_kernel(tc, x, rope_cos, rope_sin, w_words, w_sca
             return ps
 
         def project_tokens(b, c, jp, ps):
-            for jj in range(2):
-                j = 2 * jp + jj
+            for n in range(2):
+                tokens = slice((2 * jp + n) * P, (2 * jp + n + 1) * P)
                 for g in range(PASSES):
                     codes, scales = w_operand(g, c, 2)
                     nc.tensor.matmul_mx(
-                        out=ps[:, jj * 2 * HD : (jj + 1) * 2 * HD],
-                        lhsT=x_codes[b][:, g, j * P : (j + 1) * P].bitcast(E5M2X4),
-                        lhsT_scale=x_scales[b][:, g, j * P : (j + 1) * P],
+                        out=ps[:, n * 2 * HD : (n + 1) * 2 * HD],
+                        lhsT=x_codes[b][:, g, tokens].bitcast(E5M2X4),
+                        lhsT_scale=x_scales[b][:, g, tokens],
                         rhs=codes,
                         rhs_scale=scales,
                         start=(g == 0),
@@ -202,8 +199,24 @@ def tile_causalselfattention_pa_kernel(tc, x, rope_cos, rope_sin, w_words, w_sca
         def twice(ps):
             return ps[:].rearrange("p (o n) -> p o n", o=1).to_broadcast([P, 2, BANK])
 
-        def hbm_rows(b, c, count):
-            return outs[c // H][b, c % H : c % H + count].rearrange("h (p j) d -> p h (j d)", j=SLOTS)
+        def store(b, c, result):
+            count = result.shape[1]
+            rows = outs[c // H][b, c % H : c % H + count].rearrange("h (p j) d -> p h (j d)", j=SLOTS)
+            nc.sync.dma_start(out=rows, in_=result[:])
+
+        def multiply_features(c, ps):
+            products = work.tile([P, 2, T], F32, name="feature_products", bufs=6)
+            nc.vector.scalar_tensor_tensor(
+                out=products[:], in0=twice(ps), scalar=bias_cols[:, c : c + 1], in1=table_features[:], op0=ALU.add, op1=ALU.mult
+            )
+            return products
+
+        def sum_on_pe(products, ps, result):
+            for j in range(SLOTS):
+                cols = slice(j * P, (j + 1) * P)
+                nc.tensor.matmul(ps[:, cols], lhsT=products[:, 0, cols], rhs=ident[:], is_transpose=True, start=True, stop=False)
+                nc.tensor.matmul(ps[:, cols], lhsT=products[:, 1, cols], rhs=half_swap[:], is_transpose=True, start=False, stop=True)
+            nc.scalar.copy(out=result, in_=ps[:])
 
         def add_bias(c, ps):
             biased = work.tile([P, T], F32, name="biased", bufs=4)
@@ -215,84 +228,65 @@ def tile_causalselfattention_pa_kernel(tc, x, rope_cos, rope_sin, w_words, w_sca
                 nc.tensor.transpose(ps[:, j * P : (j + 1) * P], biased[:, j * P : (j + 1) * P], ident[:])
             return ps
 
-        def rotate_tokens(b, c, banks):
-            products = work.tile([P, 2, 2, T], F32, name="products", bufs=3)
+        def rotate_on_gpsimd(b, c, banks):
+            products = work.tile([P, 2, 2, T], F32, name="token_products", bufs=3)
             for n in range(2):
                 nc.vector.tensor_tensor(out=products[:, :, n, :], in0=twice(banks[n]), in1=table[:], op=ALU.mult)
-            result = work.tile([P, 2, T], F32, name="rope_result", bufs=3)
+            result = work.tile([P, 2, T], F32, name="rotated", bufs=3)
             rows = result[:].rearrange("p h (j d) -> p (h j) d", d=HD)
             with_cos = products[:, 0, :, :].rearrange("p h (j d) -> p (h j) d", d=HD)
             with_sin = products[:, 1, :, :].rearrange("p h (j d) -> p (h j) d", d=HD)
             nc.gpsimd.tensor_tensor(out=rows[:, :, 0:HALF], in0=with_cos[:, :, 0:HALF], in1=with_sin[:, :, HALF:HD], op=ALU.add)
             nc.gpsimd.tensor_tensor(out=rows[:, :, HALF:HD], in0=with_cos[:, :, HALF:HD], in1=with_sin[:, :, 0:HALF], op=ALU.add)
-            nc.sync.dma_start(out=hbm_rows(b, c, 2), in_=result[:])
-
-        def multiply_features(c, ps):
-            products = work.tile([P, 2, T], F32, name="feature_products", bufs=6)
-            nc.vector.scalar_tensor_tensor(
-                out=products[:], in0=twice(ps), scalar=bias_cols[:, c : c + 1], in1=table_features[:], op0=ALU.add, op1=ALU.mult
-            )
-            return products
-
-        def sum_to_tokens(products, ps, result):
-            for j in range(SLOTS):
-                cols = slice(j * P, (j + 1) * P)
-                nc.tensor.matmul(ps[:, cols], lhsT=products[:, 0, cols], rhs=ident[:], is_transpose=True, start=True, stop=False)
-                nc.tensor.matmul(ps[:, cols], lhsT=products[:, 1, cols], rhs=half_swap[:], is_transpose=True, start=False, stop=True)
-            nc.scalar.copy(out=result, in_=ps[:])
-
-        def by_slot(tile):
-            return tile[:].rearrange("p h (j d) -> p j h d", d=HD)
-
-        def slots_of(ps):
-            return ps[:].rearrange("p (j h d) -> p j h d", j=2, h=2)
-
-        def pair_bias(c):
-            half, n = divmod(c - V0, QUAD)
-            return v_bias[half][:, n * HD : (n + 2) * HD]
+            store(b, c, result)
 
         def v_pair(b, c, on_gpsimd):
+            half, n = divmod(c - V0, QUAD)
+            bias = v_bias[half][:, n * HD : (n + 2) * HD]
             result = work.tile([P, 2, T], F32, name="v_result", bufs=3)
-            banks = []
             if on_gpsimd:
                 plain = work.tile([P, 2, T], F32, name="v_plain", bufs=2)
+            banks = []
+
+            def slots(tile, jp):
+                return tile[:].rearrange("p h (j d) -> p j h d", d=HD)[:, 2 * jp : 2 * jp + 2, :, :]
 
             def project(jp):
-                banks.append(project_tokens(b, c, jp, bank("v", jp)))
+                banks.append(project_tokens(b, c, jp, bank("v", jp))[:].rearrange("p (j h d) -> p j h d", j=2, h=2))
                 if on_gpsimd:
-                    nc.scalar.copy(out=by_slot(plain)[:, 2 * jp : 2 * jp + 2, :, :], in_=slots_of(banks[jp]))
+                    nc.scalar.copy(out=slots(plain, jp), in_=banks[jp])
 
             def finish():
                 if on_gpsimd:
                     nc.gpsimd.tensor_tensor(
                         out=result[:].rearrange("p h (j d) -> p h j d", d=HD),
                         in0=plain[:].rearrange("p h (j d) -> p h j d", d=HD),
-                        in1=pair_bias(c).rearrange("p (h o d) -> p h o d", h=2, o=1).to_broadcast([P, 2, SLOTS, HD]),
+                        in1=bias.rearrange("p (h o d) -> p h o d", h=2, o=1).to_broadcast([P, 2, SLOTS, HD]),
                         op=ALU.add,
                     )
                 else:
-                    bias = pair_bias(c).rearrange("p (o h d) -> p o h d", o=1, h=2).to_broadcast([P, 2, 2, HD])
+                    spread_bias = bias.rearrange("p (o h d) -> p o h d", o=1, h=2).to_broadcast([P, 2, 2, HD])
                     for jp in range(2):
-                        nc.vector.tensor_tensor(out=by_slot(result)[:, 2 * jp : 2 * jp + 2, :, :], in0=slots_of(banks[jp]), in1=bias, op=ALU.add)
-                nc.sync.dma_start(out=hbm_rows(b, c, 2), in_=result[:])
+                        nc.vector.tensor_tensor(out=slots(result, jp), in0=banks[jp], in1=spread_bias, op=ALU.add)
+                store(b, c, result)
 
             return project, finish
 
-        last = B * ROUNDS - 1
-        v_pairs = [(b, V0 + 2 * i) for b in range(B) for i in range(ROUNDS)]
+        v_pairs = [(b, V0 + 2 * i) for b in range(B) for i in range(STEPS)]
         waiting = []
-        for step in range(last):
-            b, i = divmod(step, ROUNDS)
-            c0 = ROPE_QUADS[i]
-            project_v, finish_v = v_pair(*v_pairs.pop(0), step in GPSIMD_V_STEPS)
+        for step in range(B * STEPS - 1):
+            b, i = divmod(step, STEPS)
+            c0 = QUADS[i]
+            two_pairs = step == STEPS
+            project_v, finish_v = v_pair(*v_pairs.pop(0), i < X_STEPS)
             fresh = [multiply_features(c0 + n, project_features(b, c0 + n, bank("f", n))) for n in range(2)]
             project_v(0)
-            if step == DOUBLE_V_STEP:
+            if two_pairs:
                 project_v(1)
                 finish_v()
                 project_v, finish_v = v_pair(*v_pairs.pop(0), False)
-            biased = [add_bias(c0 + 2 + n, project_features(b, c0 + 2 + n, bank("mx", n))) for n in range(2)]
-            if step == DOUBLE_V_STEP:
+            biased = [add_bias(c0 + 2 + n, project_features(b, c0 + 2 + n, bank("s", n))) for n in range(2)]
+            if two_pairs:
                 project_v(0)
             project_v(1)
 
@@ -302,28 +296,28 @@ def tile_causalselfattention_pa_kernel(tc, x, rope_cos, rope_sin, w_words, w_sca
             for n in range(2):
                 t_banks.append(to_tokens(biased[n], bank("t", n)))
                 if waiting:
-                    sum_to_tokens(waiting[n], bank("mx", n), summed[:, n, :])
+                    sum_on_pe(waiting[n], bank("s", n), summed[:, n, :])
             if waiting:
-                nc.sync.dma_start(out=hbm_rows(*waiting_rows, 2), in_=summed[:])
-            waiting, waiting_rows = fresh, (b, c0)
-            if step in X_STEPS:
-                jp = X_STEPS.index(step)
-                for jj in range(2):
-                    transpose_x(x_second[jp][:, jj, :], 2 * jp + jj, grouped_second, bank("v", jj), nc.scalar.copy)
+                store(*waiting_at, summed)
+            waiting, waiting_at = fresh, (b, c0)
+            if step < X_STEPS:
+                for n in range(2):
+                    j = 2 * step + n
+                    transpose_x(x_second[step][:, n, :], as_words(grouped_second)[:, :, j * P : (j + 1) * P, :], bank("v", n), nc.scalar.copy)
             finish_v()
-            if step == QUANT_STEP:
+            if step == X_STEPS:
                 nc.vector.quantize_mx(
                     out=x_codes[1][:].rearrange("p g r -> p (g r)").bitcast(E5M2X4),
                     scales=x_scales[1][:].rearrange("p g r -> p (g r)"),
                     in_=grouped_second[:].rearrange("p g n -> p (g n)"),
                 )
-            rotate_tokens(b, c0 + 2, t_banks)
+            rotate_on_gpsimd(b, c0 + 2, t_banks)
 
-        b, c0 = B - 1, ROPE_QUADS[-1]
+        b, c0 = B - 1, QUADS[-1]
         places = [("f", 0), ("f", 1), ("v", 0), ("v", 1)]
         fresh = [multiply_features(c0 + n, project_features(b, c0 + n, bank(*places[n]))) for n in range(QUAD)]
-        heads = [(waiting_rows[1] + n, waiting[n], ("mx", n)) for n in range(2)] + [(c0 + n, fresh[n], places[n]) for n in range(QUAD)]
+        heads = [(waiting_at[1] + n, waiting[n], ("s", n)) for n in range(2)] + [(c0 + n, fresh[n], places[n]) for n in range(QUAD)]
         for c, products, place in heads:
             summed_head = work.tile([P, 1, T], F32, name="summed_head", bufs=len(heads))
-            sum_to_tokens(products, bank(*place), summed_head[:, 0, :])
-            nc.sync.dma_start(out=hbm_rows(b, c, 1), in_=summed_head[:])
+            sum_on_pe(products, bank(*place), summed_head[:, 0, :])
+            store(b, c, summed_head)

@@ -20,9 +20,9 @@ ACT = mybir.ActivationFunctionType
 P = 128
 PACK = 4
 PASSES = D // (P * PACK)
-WORDS = D // PASSES // 2
 SLOTS = T // P
 BANK = 512
+ALIGN = 256
 W_BYTES = 2 * HD
 HEADS = 3 * H
 V0 = 2 * H
@@ -52,7 +52,7 @@ def tile_causalselfattention_pa_kernel(tc, x, rope_cos, rope_sin, w_words, w_sca
         nc.scalar.dma_start(out=bias_rows[0:H, :, :], in_=qkv_b.rearrange("(s h d) -> h s d", s=3, h=H))
         planes = []
         for n, (lo, hi) in enumerate(PLANE_HEADS):
-            plane = keep.tile([P, PASSES, (hi - lo) * HD], U8, name=f"plane{n}", align_bytes=64)
+            plane = keep.tile([P, PASSES, (hi - lo) * HD], U8, name=f"plane{n}", align_bytes=ALIGN)
             nc.vector.memset(plane[:].rearrange("p g n -> p (g n)").bitcast(I32), 0)
             planes.append(plane)
         ident = keep.tile([P, P], F32, name="ident")
@@ -79,7 +79,7 @@ def tile_causalselfattention_pa_kernel(tc, x, rope_cos, rope_sin, w_words, w_sca
         w_tiles = {}
 
         def load_w(c0):
-            w_tiles[c0] = keep.tile([P, PASSES, QUAD * W_BYTES], U8, name=f"w{c0}", align_bytes=64)
+            w_tiles[c0] = keep.tile([P, PASSES, QUAD * W_BYTES], U8, name=f"w{c0}", align_bytes=ALIGN)
             nc.sync.dma_start(
                 out=w_tiles[c0][:].bitcast(I32),
                 in_=w_words[:, :, c0 * W_BYTES : (c0 + QUAD) * W_BYTES].rearrange("g p n -> p g n").bitcast(I32),
@@ -93,43 +93,38 @@ def tile_causalselfattention_pa_kernel(tc, x, rope_cos, rope_sin, w_words, w_sca
             return codes, planes[n][:, g, (c - lo) * HD : (c - lo + count) * HD]
 
         x_first = [load_x(0, j, 1) for j in range(SLOTS)]
+        load_w(QUADS[0])
+        load_scales(0)
+        load_w(V0)
         table = keep.tile([P, 2, SLOTS * HD], BF16, name="table")
         sin_raw = keep.tile([P, SLOTS, HD], BF16, name="sin_raw")
         nc.sync.dma_start(out=sin_raw[:], in_=rope_sin[0, 0].rearrange("(p j) d -> p j d", j=SLOTS))
         nc.sync.dma_start(out=table[:, 0, :], in_=rope_cos[0, 0].rearrange("(p j) d -> p (j d)", j=SLOTS))
-        load_scales(0)
-        load_w(QUADS[0])
-        load_w(V0)
-        x_second = [load_x(1, 0, 2)]
+        x_second = [load_x(1, j, 2) for j in (0, 2)]
         load_scales(1)
-        load_scales(2)
         load_w(QUADS[1])
-        x_second.append(load_x(1, 2, 2))
+        load_scales(2)
         load_w(QUADS[2])
         load_w(V0 + QUAD)
         load_w(QUADS[3])
 
-        cols_ps = bank("s", 0)
-        for s in range(3):
-            nc.tensor.matmul(cols_ps[:, s * H : (s + 1) * H], lhsT=bias_rows[:, s, :], rhs=ident_bf[:, 0:H], start=True, stop=True)
-        bias_cols = keep.tile([P, HEADS], F32, name="bias_cols")
-        nc.vector.tensor_copy(out=bias_cols[:], in_=cols_ps[:, 0:HEADS])
+        x_codes = [keep.tile([P, PASSES, T], U32, name=f"x_codes{b}", align_bytes=ALIGN) for b in range(B)]
+        x_scales = [keep.tile([P, PASSES, T], U8, name=f"x_scales{b}", align_bytes=ALIGN) for b in range(B)]
 
-        x_codes = [keep.tile([P, PASSES, T], U32, name=f"x_codes{b}", align_bytes=64) for b in range(B)]
-        x_scales = [keep.tile([P, PASSES, T], U8, name=f"x_scales{b}", align_bytes=64) for b in range(B)]
+        def by_parity(raw):
+            return raw[:].bitcast(F32).rearrange("r j (g p u) -> r (j g) u p", g=PASSES, u=2)
 
-        def transpose_x(rows, grouped, ps, copy):
-            words = rows.bitcast(F32)
+        def transpose_x(words, grouped, ps, copy):
             for g in range(PASSES):
                 for u in range(2):
                     n = 2 * g + u
-                    nc.tensor.transpose(ps[:, n * P : (n + 1) * P], words[:, WORDS * g + u : WORDS * (g + 1) : 2], ident[:])
+                    nc.tensor.transpose(ps[:, n * P : (n + 1) * P], words[:, g, u, :], ident[:])
             copy(out=grouped, in_=ps[:].rearrange("p (g u r) -> p g r u", g=PASSES, u=2))
 
         def as_words(grouped):
             return grouped[:].bitcast(F32).rearrange("p g (r u) -> p g r u", u=2)
 
-        grouped_first = [keep.tile([P, PASSES, P * PACK], BF16, name=f"grouped0_{j}", align_bytes=64) for j in range(SLOTS)]
+        grouped_first = [keep.tile([P, PASSES, P * PACK], BF16, name=f"grouped0_{j}", align_bytes=ALIGN) for j in range(SLOTS)]
 
         def quantize_first(j):
             cols = slice(j * P, (j + 1) * P)
@@ -139,26 +134,25 @@ def tile_causalselfattention_pa_kernel(tc, x, rope_cos, rope_sin, w_words, w_sca
                 )
 
         for j in range(SLOTS):
-            copy = nc.scalar.copy if j % 2 else nc.vector.tensor_copy
-            transpose_x(x_first[j][:, 0, :], as_words(grouped_first[j]), bank("t" if j % 2 else "f", j // 2), copy)
-            if j > 0:
-                quantize_first(j - 1)
-            if j == 1:
-                swapped = table[:, 1, :].rearrange("p (j d) -> p j d", d=HD)
-                nc.scalar.copy(out=swapped[:, :, 0:HALF], in_=sin_raw[:, :, HALF:HD])
-                nc.scalar.activation(out=swapped[:, :, HALF:HD], in_=sin_raw[:, :, 0:HALF], func=ACT.Copy, scale=-1.0)
-        quantize_first(SLOTS - 1)
-        grouped_second = keep.tile([P, PASSES, T * PACK], BF16, name="grouped1", align_bytes=64)
+            words = keep.tile([P, PASSES, 2, P], F32, name=f"x_sorted0_{j}", align_bytes=ALIGN)
+            nc.vector.tensor_copy(out=words[:], in_=by_parity(x_first[j]))
+            transpose_x(words, as_words(grouped_first[j]), bank("ft"[j % 2], j // 2), nc.scalar.copy)
+        for j in range(SLOTS):
+            quantize_first(j)
+        swapped = table[:, 1, :].rearrange("p (j d) -> p j d", d=HD)
+        nc.vector.tensor_copy(out=swapped[:, :, 0:HALF], in_=sin_raw[:, :, HALF:HD])
+        nc.vector.tensor_scalar(out=swapped[:, :, HALF:HD], in0=sin_raw[:, :, 0:HALF], scalar1=-1.0, scalar2=None, op0=ALU.mult)
+        grouped_second = keep.tile([P, PASSES, T * PACK], BF16, name="grouped1", align_bytes=ALIGN)
 
-        table_ps = psum.tile([P, 2, T], BF16, tag="s1", name="table_ps")
-        for n in range(2):
-            for j in range(SLOTS):
-                nc.tensor.transpose(table_ps[:, n, j * P : (j + 1) * P], table[:, n, j * HD : (j + 1) * HD], ident_bf[:])
-        table_features = keep.tile([P, 2, T], BF16, name="table_features")
-        nc.scalar.copy(out=table_features[:], in_=table_ps[:])
+        cols_ps = bank("s", 0)
+        for s in range(2):
+            nc.tensor.matmul(cols_ps[:, s * H : (s + 1) * H], lhsT=bias_rows[:, s, :], rhs=ident_bf[:, 0:H], start=True, stop=True)
+        bias_cols = keep.tile([P, V0], F32, name="bias_cols")
+        nc.scalar.copy(out=bias_cols[:], in_=cols_ps[:, 0:V0])
+
         v_bias = []
-        for half in range(2):
-            spread = bank("t", half)
+        for half, place in enumerate((("s", 1), ("v", 0))):
+            spread = bank(*place)
             for n in range(QUAD):
                 h = half * QUAD + n
                 picker = ident_bf[:, h : h + 1].to_broadcast([P, P])
@@ -205,7 +199,7 @@ def tile_causalselfattention_pa_kernel(tc, x, rope_cos, rope_sin, w_words, w_sca
             nc.sync.dma_start(out=rows, in_=result[:])
 
         def multiply_features(c, ps):
-            products = work.tile([P, 2, T], F32, name="feature_products", bufs=6)
+            products = work.tile([P, 2, T], F32, name="feature_products", bufs=6, align_bytes=ALIGN)
             nc.vector.scalar_tensor_tensor(
                 out=products[:], in0=twice(ps), scalar=bias_cols[:, c : c + 1], in1=table_features[:], op0=ALU.add, op1=ALU.mult
             )
@@ -219,7 +213,7 @@ def tile_causalselfattention_pa_kernel(tc, x, rope_cos, rope_sin, w_words, w_sca
             nc.scalar.copy(out=result, in_=ps[:])
 
         def add_bias(c, ps):
-            biased = work.tile([P, T], F32, name="biased", bufs=4)
+            biased = work.tile([P, T], F32, name="biased", bufs=4, align_bytes=ALIGN)
             nc.scalar.activation(out=biased[:], in_=ps[:], func=ACT.Identity, bias=bias_cols[:, c : c + 1])
             return biased
 
@@ -229,10 +223,10 @@ def tile_causalselfattention_pa_kernel(tc, x, rope_cos, rope_sin, w_words, w_sca
             return ps
 
         def rotate_on_gpsimd(b, c, banks):
-            products = work.tile([P, 2, 2, T], F32, name="token_products", bufs=3)
+            products = work.tile([P, 2, 2, T], F32, name="token_products", bufs=3, align_bytes=ALIGN)
             for n in range(2):
                 nc.vector.tensor_tensor(out=products[:, :, n, :], in0=twice(banks[n]), in1=table[:], op=ALU.mult)
-            result = work.tile([P, 2, T], F32, name="rotated", bufs=3)
+            result = work.tile([P, 2, T], F32, name="rotated", bufs=3, align_bytes=ALIGN)
             rows = result[:].rearrange("p h (j d) -> p (h j) d", d=HD)
             with_cos = products[:, 0, :, :].rearrange("p h (j d) -> p (h j) d", d=HD)
             with_sin = products[:, 1, :, :].rearrange("p h (j d) -> p (h j) d", d=HD)
@@ -243,9 +237,9 @@ def tile_causalselfattention_pa_kernel(tc, x, rope_cos, rope_sin, w_words, w_sca
         def v_pair(b, c, on_gpsimd):
             half, n = divmod(c - V0, QUAD)
             bias = v_bias[half][:, n * HD : (n + 2) * HD]
-            result = work.tile([P, 2, T], F32, name="v_result", bufs=3)
+            result = work.tile([P, 2, T], F32, name="v_result", bufs=3, align_bytes=ALIGN)
             if on_gpsimd:
-                plain = work.tile([P, 2, T], F32, name="v_plain", bufs=2)
+                plain = work.tile([P, 2, T], F32, name="v_plain", bufs=2, align_bytes=ALIGN)
             banks = []
 
             def slots(tile, jp):
@@ -279,7 +273,18 @@ def tile_causalselfattention_pa_kernel(tc, x, rope_cos, rope_sin, w_words, w_sca
             c0 = QUADS[i]
             two_pairs = step == STEPS
             project_v, finish_v = v_pair(*v_pairs.pop(0), i < X_STEPS)
-            fresh = [multiply_features(c0 + n, project_features(b, c0 + n, bank("f", n))) for n in range(2)]
+            f_banks = [project_features(b, c0 + n, bank("f", n)) for n in range(2)]
+            if step == 0:
+                x_sorted = [keep.tile([P, 2 * PASSES, 2, P], F32, name=f"x_sorted{n}", align_bytes=ALIGN) for n in range(X_STEPS)]
+                for n in range(X_STEPS):
+                    nc.vector.tensor_copy(out=x_sorted[n][:], in_=by_parity(x_second[n]))
+                table_ps = psum.tile([P, 2, T], BF16, tag="v1", name="table_ps")
+                for n in range(2):
+                    for j in range(SLOTS):
+                        nc.tensor.transpose(table_ps[:, n, j * P : (j + 1) * P], table[:, n, j * HD : (j + 1) * HD], ident_bf[:])
+                table_features = keep.tile([P, 2, T], BF16, name="table_features")
+                nc.scalar.copy(out=table_features[:], in_=table_ps[:])
+            fresh = [multiply_features(c0 + n, f_banks[n]) for n in range(2)]
             project_v(0)
             if two_pairs:
                 project_v(1)
@@ -292,7 +297,7 @@ def tile_causalselfattention_pa_kernel(tc, x, rope_cos, rope_sin, w_words, w_sca
 
             t_banks = []
             if waiting:
-                summed = work.tile([P, 2, T], F32, name="summed", bufs=3)
+                summed = work.tile([P, 2, T], F32, name="summed", bufs=3, align_bytes=ALIGN)
             for n in range(2):
                 t_banks.append(to_tokens(biased[n], bank("t", n)))
                 if waiting:
@@ -303,7 +308,8 @@ def tile_causalselfattention_pa_kernel(tc, x, rope_cos, rope_sin, w_words, w_sca
             if step < X_STEPS:
                 for n in range(2):
                     j = 2 * step + n
-                    transpose_x(x_second[step][:, n, :], as_words(grouped_second)[:, :, j * P : (j + 1) * P, :], bank("v", n), nc.scalar.copy)
+                    words = x_sorted[step][:, n * PASSES : (n + 1) * PASSES, :, :]
+                    transpose_x(words, as_words(grouped_second)[:, :, j * P : (j + 1) * P, :], bank("v", n), nc.scalar.copy)
             finish_v()
             if step == X_STEPS:
                 nc.vector.quantize_mx(
@@ -318,6 +324,6 @@ def tile_causalselfattention_pa_kernel(tc, x, rope_cos, rope_sin, w_words, w_sca
         fresh = [multiply_features(c0 + n, project_features(b, c0 + n, bank(*places[n]))) for n in range(QUAD)]
         heads = [(waiting_at[1] + n, waiting[n], ("s", n)) for n in range(2)] + [(c0 + n, fresh[n], places[n]) for n in range(QUAD)]
         for c, products, place in heads:
-            summed_head = work.tile([P, 1, T], F32, name="summed_head", bufs=len(heads))
+            summed_head = work.tile([P, 1, T], F32, name="summed_head", bufs=len(heads), align_bytes=ALIGN)
             sum_on_pe(products, bank(*place), summed_head[:, 0, :])
             store(b, c, summed_head)

from contextlib import ExitStack

import concourse.mybir as mybir
from concourse.masks import make_identity

B, T, D, H, HD = 2, 512, 1024, 8, 128
HALF = HD // 2
FLOPS = 2 * B * T * D * 3 * H * HD

F32 = mybir.dt.float32
BF16 = mybir.dt.bfloat16
I32 = mybir.dt.int32
U32 = mybir.dt.uint32
U8 = mybir.dt.uint8
E5M2X4 = mybir.dt.float8_e5m2_x4
E2M1X4 = mybir.dt.float4_e2m1fn_x4
ALU = mybir.AluOpType
ACT = mybir.ActivationFunctionType

P = 128
PACK = 4
PASSES = D // (P * PACK)
SLOTS = T // P
BANK = 512
ALIGN = 256
W_BYTES = 2 * HD
HEADS = 3 * H
V0 = 2 * H
QUAD = 4
STEPS = V0 // QUAD
FIRST = V0 - QUAD
QUADS = [FIRST] + list(range(0, FIRST, QUAD))
PLANE_HEADS = [(FIRST, V0 + 2), (0, FIRST), (V0 + 2, HEADS)]
X_STEPS = 2


def tile_causalselfattention_pa_kernel(tc, x, rope_cos, rope_sin, w_words, w_scales, qkv_b, out_0, out_1, out_2):
    nc = tc.nc
    outs = (out_0, out_1, out_2)

    with ExitStack() as ctx:
        keep = ctx.enter_context(tc.tile_pool(name="keep", bufs=1))
        work = ctx.enter_context(tc.tile_pool(name="work", bufs=1))
        psum = ctx.enter_context(tc.psum_pool(name="psum", bufs=1))
        ctx.enter_context(tc.manual_schedule())

        def bank(role, n):
            return psum.tile([P, BANK], F32, tag=f"{role}{n}", name=f"{role}{n}")

        bias_rows = keep.tile([P, 3, HD], BF16, name="bias_rows")
        nc.gpsimd.memset(bias_rows[:].rearrange("p s d -> p (s d)").bitcast(I32), 0)
        nc.scalar.dma_start(out=bias_rows[0:H, :, :], in_=qkv_b.rearrange("(s h d) -> h s d", s=3, h=H))
        planes = []
        for n, (lo, hi) in enumerate(PLANE_HEADS):
            plane = keep.tile([P, PASSES, (hi - lo) * HD], U8, name=f"plane{n}", align_bytes=ALIGN)
            nc.vector.memset(plane[:].rearrange("p g n -> p (g n)").bitcast(I32), 0)
            planes.append(plane)
        ident = keep.tile([P, P], F32, name="ident")
        make_identity(nc, ident[:])
        ident_bf = keep.tile([P, P], BF16, name="ident_bf")
        make_identity(nc, ident_bf[:])
        half_swap = keep.tile([P, P], F32, name="half_swap")
        nc.scalar.copy(out=half_swap[:, 0:HALF], in_=ident[:, HALF:HD])
        nc.scalar.copy(out=half_swap[:, HALF:HD], in_=ident[:, 0:HALF])

        def load_x(b, j, count):
            raw = keep.tile([P, count, D], BF16, name=f"x_raw{b}_{j}")
            nc.sync.dma_start(out=raw[:], in_=x[b].rearrange("(p j) k -> p j k", j=SLOTS)[:, j : j + count, :])
            return raw

        def load_scales(n):
            lo, hi = PLANE_HEADS[n]
            for r in range(4):
                nc.sync.dma_start(
                    out=planes[n][r:P:32, :, :].bitcast(I32),
                    in_=w_scales[:, r:16:4, lo * HD : hi * HD].rearrange("g q n -> q g n").bitcast(I32),
                )

        w_tiles = {}

        def load_w(c0):
            w_tiles[c0] = keep.tile([P, PASSES, QUAD * W_BYTES], U8, name=f"w{c0}", align_bytes=ALIGN)
            nc.sync.dma_start(
                out=w_tiles[c0][:].bitcast(I32),
                in_=w_words[:, :, c0 * W_BYTES : (c0 + QUAD) * W_BYTES].rearrange("g p n -> p g n").bitcast(I32),
            )

        def w_operand(g, c, count):
            c0 = c - c % QUAD
            n = [lo <= c < hi for lo, hi in PLANE_HEADS].index(True)
            lo = PLANE_HEADS[n][0]
            codes = w_tiles[c0][:, g, (c - c0) * W_BYTES : (c - c0 + count) * W_BYTES].bitcast(E2M1X4)
            return codes, planes[n][:, g, (c - lo) * HD : (c - lo + count) * HD]

        x_first = [load_x(0, j, 1) for j in range(SLOTS)]
        load_w(QUADS[0])
        load_scales(0)
        load_w(V0)
        table = keep.tile([P, 2, SLOTS * HD], BF16, name="table")
        sin_raw = keep.tile([P, SLOTS, HD], BF16, name="sin_raw")
        nc.sync.dma_start(out=sin_raw[:], in_=rope_sin[0, 0].rearrange("(p j) d -> p j d", j=SLOTS))
        nc.sync.dma_start(out=table[:, 0, :], in_=rope_cos[0, 0].rearrange("(p j) d -> p (j d)", j=SLOTS))
        x_second = [load_x(1, j, 2) for j in (0, 2)]
        load_scales(1)
        load_w(QUADS[1])
        load_scales(2)
        load_w(QUADS[2])
        load_w(V0 + QUAD)
        load_w(QUADS[3])

        x_codes = [keep.tile([P, PASSES, T], U32, name=f"x_codes{b}", align_bytes=ALIGN) for b in range(B)]
        x_scales = [keep.tile([P, PASSES, T], U8, name=f"x_scales{b}", align_bytes=ALIGN) for b in range(B)]

        def by_parity(raw):
            return raw[:].bitcast(F32).rearrange("r j (g p u) -> r (j g) u p", g=PASSES, u=2)

        def transpose_x(words, grouped, ps, copy):
            for g in range(PASSES):
                for u in range(2):
                    n = 2 * g + u
                    nc.tensor.transpose(ps[:, n * P : (n + 1) * P], words[:, g, u, :], ident[:])
            copy(out=grouped, in_=ps[:].rearrange("p (g u r) -> p g r u", g=PASSES, u=2))

        def as_words(grouped):
            return grouped[:].bitcast(F32).rearrange("p g (r u) -> p g r u", u=2)

        grouped_first = [keep.tile([P, PASSES, P * PACK], BF16, name=f"grouped0_{j}", align_bytes=ALIGN) for j in range(SLOTS)]

        def quantize_first(j):
            cols = slice(j * P, (j + 1) * P)
            for g in range(PASSES):
                nc.vector.quantize_mx(
                    out=x_codes[0][:, g, cols].bitcast(E5M2X4), scales=x_scales[0][:, g, cols], in_=grouped_first[j][:, g, :]
                )

        for j in range(SLOTS):
            words = keep.tile([P, PASSES, 2, P], F32, name=f"x_sorted0_{j}", align_bytes=ALIGN)
            nc.vector.tensor_copy(out=words[:], in_=by_parity(x_first[j]))
            transpose_x(words, as_words(grouped_first[j]), bank("ft"[j % 2], j // 2), nc.scalar.copy)
        for j in range(SLOTS):
            quantize_first(j)
        swapped = table[:, 1, :].rearrange("p (j d) -> p j d", d=HD)
        nc.vector.tensor_copy(out=swapped[:, :, 0:HALF], in_=sin_raw[:, :, HALF:HD])
        nc.vector.tensor_scalar(out=swapped[:, :, HALF:HD], in0=sin_raw[:, :, 0:HALF], scalar1=-1.0, scalar2=None, op0=ALU.mult)
        grouped_second = keep.tile([P, PASSES, T * PACK], BF16, name="grouped1", align_bytes=ALIGN)

        cols_ps = bank("s", 0)
        for s in range(2):
            nc.tensor.matmul(cols_ps[:, s * H : (s + 1) * H], lhsT=bias_rows[:, s, :], rhs=ident_bf[:, 0:H], start=True, stop=True)
        bias_cols = keep.tile([P, V0], F32, name="bias_cols")
        nc.scalar.copy(out=bias_cols[:], in_=cols_ps[:, 0:V0])

        v_bias = []
        for half, place in enumerate((("s", 1), ("v", 0))):
            spread = bank(*place)
            for n in range(QUAD):
                h = half * QUAD + n
                picker = ident_bf[:, h : h + 1].to_broadcast([P, P])
                nc.tensor.matmul(spread[:, n * HD : (n + 1) * HD], lhsT=picker, rhs=bias_rows[:, 2, :], start=True, stop=True)
            v_bias.append(keep.tile([P, QUAD * HD], F32, name=f"v_bias{half}"))
            nc.scalar.copy(out=v_bias[half][:], in_=spread[:])

        def project_features(b, c, ps):
            for g in range(PASSES):
                codes, scales = w_operand(g, c, 1)
                nc.tensor.matmul_mx(
                    out=ps[:],
                    lhsT=codes,
                    lhsT_scale=scales,
                    rhs=x_codes[b][:, g, :].bitcast(E5M2X4),
                    rhs_scale=x_scales[b][:, g, :],
                    start=(g == 0),
                    stop=(g == PASSES - 1),
                )
            return ps

        def project_tokens(b, c, jp, ps):
            for n in range(2):
                tokens = slice((2 * jp + n) * P, (2 * jp + n + 1) * P)
                for g in range(PASSES):
                    codes, scales = w_operand(g, c, 2)
                    nc.tensor.matmul_mx(
                        out=ps[:, n * 2 * HD : (n + 1) * 2 * HD],
                        lhsT=x_codes[b][:, g, tokens].bitcast(E5M2X4),
                        lhsT_scale=x_scales[b][:, g, tokens],
                        rhs=codes,
                        rhs_scale=scales,
                        start=(g == 0),
                        stop=(g == PASSES - 1),
                    )
            return ps

        def twice(ps):
            return ps[:].rearrange("p (o n) -> p o n", o=1).to_broadcast([P, 2, BANK])

        def store(b, c, result):
            count = result.shape[1]
            rows = outs[c // H][b, c % H : c % H + count].rearrange("h (p j) d -> p h (j d)", j=SLOTS)
            nc.sync.dma_start(out=rows, in_=result[:])

        def multiply_features(c, ps):
            products = work.tile([P, 2, T], F32, name="feature_products", bufs=6, align_bytes=ALIGN)
            nc.vector.scalar_tensor_tensor(
                out=products[:], in0=twice(ps), scalar=bias_cols[:, c : c + 1], in1=table_features[:], op0=ALU.add, op1=ALU.mult
            )
            return products

        def sum_on_pe(products, ps, result):
            for j in range(SLOTS):
                cols = slice(j * P, (j + 1) * P)
                nc.tensor.matmul(ps[:, cols], lhsT=products[:, 0, cols], rhs=ident[:], is_transpose=True, start=True, stop=False)
                nc.tensor.matmul(ps[:, cols], lhsT=products[:, 1, cols], rhs=half_swap[:], is_transpose=True, start=False, stop=True)
            nc.scalar.copy(out=result, in_=ps[:])

        def add_bias(c, ps):
            biased = work.tile([P, T], F32, name="biased", bufs=4, align_bytes=ALIGN)
            nc.scalar.activation(out=biased[:], in_=ps[:], func=ACT.Identity, bias=bias_cols[:, c : c + 1])
            return biased

        def to_tokens(biased, ps):
            for j in range(SLOTS):
                nc.tensor.transpose(ps[:, j * P : (j + 1) * P], biased[:, j * P : (j + 1) * P], ident[:])
            return ps

        def rotate_on_gpsimd(b, c, banks):
            products = work.tile([P, 2, 2, T], F32, name="token_products", bufs=3, align_bytes=ALIGN)
            for n in range(2):
                nc.vector.tensor_tensor(out=products[:, :, n, :], in0=twice(banks[n]), in1=table[:], op=ALU.mult)
            result = work.tile([P, 2, T], F32, name="rotated", bufs=3, align_bytes=ALIGN)
            rows = result[:].rearrange("p h (j d) -> p (h j) d", d=HD)
            with_cos = products[:, 0, :, :].rearrange("p h (j d) -> p (h j) d", d=HD)
            with_sin = products[:, 1, :, :].rearrange("p h (j d) -> p (h j) d", d=HD)
            nc.gpsimd.tensor_tensor(out=rows[:, :, 0:HALF], in0=with_cos[:, :, 0:HALF], in1=with_sin[:, :, HALF:HD], op=ALU.add)
            nc.gpsimd.tensor_tensor(out=rows[:, :, HALF:HD], in0=with_cos[:, :, HALF:HD], in1=with_sin[:, :, 0:HALF], op=ALU.add)
            store(b, c, result)

        def v_pair(b, c, on_gpsimd):
            half, n = divmod(c - V0, QUAD)
            bias = v_bias[half][:, n * HD : (n + 2) * HD]
            result = work.tile([P, 2, T], F32, name="v_result", bufs=3, align_bytes=ALIGN)
            if on_gpsimd:
                plain = work.tile([P, 2, T], F32, name="v_plain", bufs=2, align_bytes=ALIGN)
            banks = []

            def slots(tile, jp):
                return tile[:].rearrange("p h (j d) -> p j h d", d=HD)[:, 2 * jp : 2 * jp + 2, :, :]

            def project(jp):
                banks.append(project_tokens(b, c, jp, bank("v", jp))[:].rearrange("p (j h d) -> p j h d", j=2, h=2))
                if on_gpsimd:
                    nc.scalar.copy(out=slots(plain, jp), in_=banks[jp])

            def finish():
                if on_gpsimd:
                    nc.gpsimd.tensor_tensor(
                        out=result[:].rearrange("p h (j d) -> p h j d", d=HD),
                        in0=plain[:].rearrange("p h (j d) -> p h j d", d=HD),
                        in1=bias.rearrange("p (h o d) -> p h o d", h=2, o=1).to_broadcast([P, 2, SLOTS, HD]),
                        op=ALU.add,
                    )
                else:
                    spread_bias = bias.rearrange("p (o h d) -> p o h d", o=1, h=2).to_broadcast([P, 2, 2, HD])
                    for jp in range(2):
                        nc.vector.tensor_tensor(out=slots(result, jp), in0=banks[jp], in1=spread_bias, op=ALU.add)
                store(b, c, result)

            return project, finish

        v_pairs = [(b, V0 + 2 * i) for b in range(B) for i in range(STEPS)]
        waiting = []
        for step in range(B * STEPS - 1):
            b, i = divmod(step, STEPS)
            c0 = QUADS[i]
            two_pairs = step == STEPS
            project_v, finish_v = v_pair(*v_pairs.pop(0), i < X_STEPS)
            f_banks = [project_features(b, c0 + n, bank("f", n)) for n in range(2)]
            if step == 0:
                x_sorted = [keep.tile([P, 2 * PASSES, 2, P], F32, name=f"x_sorted{n}", align_bytes=ALIGN) for n in range(X_STEPS)]
                for n in range(X_STEPS):
                    nc.vector.tensor_copy(out=x_sorted[n][:], in_=by_parity(x_second[n]))
                table_ps = psum.tile([P, 2, T], BF16, tag="v1", name="table_ps")
                for n in range(2):
                    for j in range(SLOTS):
                        nc.tensor.transpose(table_ps[:, n, j * P : (j + 1) * P], table[:, n, j * HD : (j + 1) * HD], ident_bf[:])
                table_features = keep.tile([P, 2, T], BF16, name="table_features")
                nc.scalar.copy(out=table_features[:], in_=table_ps[:])
            fresh = [multiply_features(c0 + n, f_banks[n]) for n in range(2)]
            project_v(0)
            if two_pairs:
                project_v(1)
                finish_v()
                project_v, finish_v = v_pair(*v_pairs.pop(0), False)
            biased = [add_bias(c0 + 2 + n, project_features(b, c0 + 2 + n, bank("s", n))) for n in range(2)]
            if two_pairs:
                project_v(0)
            project_v(1)

            t_banks = []
            if waiting:
                summed = work.tile([P, 2, T], F32, name="summed", bufs=3, align_bytes=ALIGN)
            for n in range(2):
                t_banks.append(to_tokens(biased[n], bank("t", n)))
                if waiting:
                    sum_on_pe(waiting[n], bank("s", n), summed[:, n, :])
            if waiting:
                store(*waiting_at, summed)
            waiting, waiting_at = fresh, (b, c0)
            if step < X_STEPS:
                for n in range(2):
                    j = 2 * step + n
                    words = x_sorted[step][:, n * PASSES : (n + 1) * PASSES, :, :]
                    transpose_x(words, as_words(grouped_second)[:, :, j * P : (j + 1) * P, :], bank("v", n), nc.scalar.copy)
            finish_v()
            if step == X_STEPS:
                nc.vector.quantize_mx(
                    out=x_codes[1][:].rearrange("p g r -> p (g r)").bitcast(E5M2X4),
                    scales=x_scales[1][:].rearrange("p g r -> p (g r)"),
                    in_=grouped_second[:].rearrange("p g n -> p (g n)"),
                )
            rotate_on_gpsimd(b, c0 + 2, t_banks)

        b, c0 = B - 1, QUADS[-1]
        places = [("f", 0), ("f", 1), ("v", 0), ("v", 1)]
        fresh = [multiply_features(c0 + n, project_features(b, c0 + n, bank(*places[n]))) for n in range(QUAD)]
        heads = [(waiting_at[1] + n, waiting[n], ("s", n)) for n in range(2)] + [(c0 + n, fresh[n], places[n]) for n in range(QUAD)]
        for c, products, place in heads:
            summed_head = work.tile([P, 1, T], F32, name="summed_head", bufs=len(heads), align_bytes=ALIGN)
            sum_on_pe(products, bank(*place), summed_head[:, 0, :])
            store(b, c, summed_head)
